import numpy as np
import ml_dtypes


def mxq(x, axis, fmt="e4m3"):
    dtype, down = {"e4m3": (ml_dtypes.float8_e4m3fn, 7), "e5m2": (ml_dtypes.float8_e5m2, 14)}[fmt]
    v = np.moveaxis(np.asarray(x, np.float32).astype(ml_dtypes.bfloat16).astype(np.float64), axis, -1)
    blocks = v.reshape(v.shape[:-1] + (-1, 32))
    amax = np.abs(blocks).max(-1, keepdims=True)
    byte = np.maximum(np.where(amax > 0, np.frexp(amax)[1] - 1 + 127, 0) - down, 1)
    scale = np.exp2(byte - 127.0)
    codes = (blocks / scale).astype(np.float32).astype(dtype).astype(np.float64)
    return np.moveaxis((codes * scale).reshape(v.shape), -1, axis)


WIDE = False


def mx_kscale(k):
    if not WIDE:
        return np.ones(k)
    levels = np.array([10, -10, 5, -5, 0])
    a = np.random.permutation(np.resize(levels, k // 512 * 4)).reshape(k // 512, 4)
    idx = np.arange(k)
    return np.exp2(a[idx // 512, idx % 128 // 32])


BF16 = ml_dtypes.bfloat16


def bf(x):
    return np.asarray(x, np.float32).astype(BF16)


def f64(x):
    return np.asarray(x).astype(np.float64)


B, M, K, N = 4, 1024, 1024, 1024
THRESHOLD = 1e-6
TILE = 64
LIVE = 4e-6
QUIET = 8e-7


def mask_inactive_tiles(a, threshold, tile=TILE):
    nb, m, k = a.shape
    blocks = np.abs(a).reshape(nb, m // tile, tile, k // tile, tile)
    active = blocks.max(axis=(2, 4)) > threshold
    mask = np.repeat(np.repeat(active, tile, axis=1), tile, axis=2)
    return a * mask.astype(a.dtype)


def setup_inputs():
    s = mx_kscale(K)
    lv = LIVE / s.min()
    live = np.random.random((B, M // TILE, K // TILE)) < 0.75
    livem = np.repeat(np.repeat(live, TILE, axis=1), TILE, axis=2)
    a_live = np.random.standard_normal((B, M, K)) * lv * s
    a_quiet = np.random.uniform(-QUIET, QUIET, (B, M, K))
    return {"a": bf(np.where(livem, a_live, a_quiet)),
            "b": bf(np.random.standard_normal((B, K, N)) / np.sqrt(K) / lv / s[:, None])}


def reference(a, b):
    a_sp = mask_inactive_tiles(f64(a), THRESHOLD)
    return mxq(a_sp, 2, "e4m3") @ mxq(f64(b), 1, "e4m3")

from contextlib import ExitStack

import concourse.mybir as mybir
from concourse.masks import make_identity

FLOPS = 2 * 4 * 1024 * 1024 * 1024

BF16 = mybir.dt.bfloat16
F32 = mybir.dt.float32
I32 = mybir.dt.int32
U32 = mybir.dt.uint32
U8 = mybir.dt.uint8
FP8X4 = mybir.dt.float8_e4m3fn_x4
ALU = mybir.AluOpType
AX = mybir.AxisListType

P = 128
NB = 4
THRESHOLD = 1e-6
PIN = False
G_COLS = 256


def tile_sparsebmm_t_kernel(tc, a, b, out):
    nc = tc.nc
    with ExitStack() as ctx:
        const = ctx.enter_context(tc.tile_pool(name="const", bufs=1))
        raw = ctx.enter_context(tc.tile_pool(name="raw", bufs=3))
        scr = ctx.enter_context(tc.tile_pool(name="scr", bufs=1))
        small = ctx.enter_context(tc.tile_pool(name="small", bufs=2))
        gap = ctx.enter_context(tc.tile_pool(name="gap", bufs=4))
        gbp = ctx.enter_context(tc.tile_pool(name="gbp", bufs=4))
        codes = ctx.enter_context(tc.tile_pool(name="codes", bufs=2))
        outp = ctx.enter_context(tc.tile_pool(name="outp", bufs=3))
        ps_xt = ctx.enter_context(tc.psum_pool(name="ps_xt", bufs=3))
        ps_acc = ctx.enter_context(tc.psum_pool(name="ps_acc", bufs=4))
        ps_cnt = ctx.enter_context(tc.psum_pool(name="ps_cnt", bufs=1))
        if PIN:
            ctx.enter_context(tc.manual_schedule())

        a_raw = []
        b_raw = []
        for i in range(NB):
            a_t = raw.tile([P, 8192], BF16, tag="a_raw", name="a_raw%d" % i)
            b_t = raw.tile([P, 8192], BF16, tag="b_raw", name="b_raw%d" % i)
            a_raw.append(a_t)
            b_raw.append(b_t)
            a_view = a[i].rearrange("(p j) k -> p (j k)", j=8)
            for c in range(2):
                nc.sync.dma_start(out=a_t[:, 4096 * c:4096 * (c + 1)], in_=a_view[:, 4096 * c:4096 * (c + 1)])
            for g in range(2):
                nc.sync.dma_start(
                    out=b_t[:, 4096 * g:4096 * (g + 1)].rearrange("q (u x) -> q u x", u=2),
                    in_=b[i][512 * g:512 * (g + 1), :].rearrange("(u q e) n -> q u (e n)", u=2, e=2),
                )

        ident = const.tile([P, P], F32)
        make_identity(nc, ident[:])
        blk = const.tile([P, 16], F32)
        nc.vector.tensor_reduce(out=blk[:], in_=ident[:].rearrange("p (g c) -> p g c", c=8), axis=AX.X, op=ALU.add)
        group_ones = const.tile([P, P], BF16)
        nc.vector.tensor_copy(
            out=group_ones[:].rearrange("p (g c) -> p g c", c=8),
            in_=blk[:].unsqueeze(2).to_broadcast([P, 16, 8]),
        )
        ind = const.tile([P, 32 * NB], BF16)
        nc.vector.memset(ind[:].bitcast(I32), 0)

        state = {}

        def absmax(i, c):
            ab = scr.tile([P, 4096], BF16, tag="ab", name="ab_%d_%d" % (i, c))
            nc.vector.tensor_scalar(
                out=ab[:].bitcast(I32),
                in0=a_raw[i][:, 4096 * c:4096 * (c + 1)].bitcast(I32),
                scalar1=0x7FFF7FFF, scalar2=None, op0=ALU.bitwise_and,
            )
            nc.vector.tensor_tensor(out=ab[:, 0:2048], in0=ab[:, 0:2048], in1=ab[:, 2048:4096], op=ALU.max)
            hm = scr.tile([P, 1024], BF16, tag="hm%d" % c, name="hm_%d_%d" % (i, c))
            state["hm", i, c] = hm
            nc.vector.tensor_tensor(out=hm[:], in0=ab[:, 0:1024], in1=ab[:, 1024:2048], op=ALU.max)

        def chain_a(i):
            h0 = state["hm", i, 0]
            nc.vector.tensor_tensor(out=h0[:], in0=h0[:], in1=state["hm", i, 1][:], op=ALU.max)
            rm = small.tile([P, 16], F32, tag="rm", name="rm_%d" % i)
            nc.vector.tensor_reduce(out=rm[:], in_=h0[:].rearrange("p (t k) -> p t k", k=64), axis=AX.X, op=ALU.max)
            nc.vector.tensor_scalar(
                out=ind[:, 32 * i:32 * i + 16], in0=rm[:], scalar1=THRESHOLD, scalar2=None, op0=ALU.is_gt
            )

        def count(i):
            cnt = ps_cnt.tile([P, 32], F32, tag="cnt", name="cnt_%d" % i)
            state["cnt", i] = cnt
            nc.tensor.matmul(out=cnt[:], lhsT=group_ones[:], rhs=ind[:, 32 * i:32 * (i + 1)], start=True, stop=True)

        def chain_b(i):
            mask = small.tile([P, 16], F32, tag="mask", name="mask_%d" % i)
            state["mask", i] = mask
            nc.vector.tensor_scalar(
                out=mask[:], in0=state["cnt", i][:, 0:16], scalar1=1.0, scalar2=None, op0=ALU.min
            )

        def mask_mul(i):
            mask = state["mask", i]
            view = a_raw[i][:].rearrange("p (j t k) -> p t j k", j=8, t=16, k=64)
            for t in range(16):
                nc.vector.tensor_scalar(
                    out=view[:, t], in0=view[:, t], scalar1=mask[:, t:t + 1], scalar2=None, op0=ALU.mult
                )

        def transposes(i, j):
            aw = a_raw[i][:].bitcast(F32)
            xt = ps_xt.tile([P, 512], F32, tag="xt", name="xt_%d_%d" % (i, j))
            state["xt", i, j] = xt
            for kc in range(4):
                nc.tensor.transpose(xt[:, 128 * kc:128 * (kc + 1)], aw[:, 512 * j + 128 * kc:512 * j + 128 * (kc + 1)], ident[:])

        def exit_a(i, j):
            if j % 2 == 0:
                ga = gap.tile([P, 2048], BF16, tag="ga", name="ga_%d_%d" % (i, j // 2), align_bytes=64)
                state["ga", i, j // 2] = ga
            ga = state["ga", i, j // 2]
            dst = ga[:].bitcast(F32)[:, 512 * (j % 2):512 * (j % 2 + 1)]
            copy = nc.vector.tensor_copy if (i == NB - 1 and j % 2 == 1) else nc.scalar.copy
            copy(
                out=dst.rearrange("p (g m u) -> p g m u", g=2, m=128, u=2),
                in_=state["xt", i, j][:].rearrange("p (g u m) -> p g m u", g=2, u=2, m=128),
            )

        def quant_a(i, c):
            if c == 0:
                state["ac", i] = codes.tile([P, 2048], U32, tag="ac", name="ac_%d" % i, align_bytes=64)
                state["asc", i] = codes.tile([P, 2048], U8, tag="asc", name="asc_%d" % i, align_bytes=64)
            nc.vector.quantize_mx(
                out=state["ac", i][:, 512 * c:512 * (c + 1)].bitcast(FP8X4),
                scales=state["asc", i][:, 512 * c:512 * (c + 1)],
                in_=state["ga", i, c][:],
            )

        def regroup(i, g, h, eng):
            if ("gb", i, g) not in state:
                state["gb", i, g] = gbp.tile([P, 4096], BF16, tag="gb", name="gb_%d_%d" % (i, g), align_bytes=64)
            gb = state["gb", i, g]
            src = b_raw[i][:, 4096 * g:4096 * (g + 1)].rearrange("q (t n) -> q t n", t=4)
            if eng == "g":
                for n0 in range(512 * h, 512 * (h + 1), G_COLS):
                    nc.gpsimd.tensor_scalar(
                        out=gb[:, 4 * n0:4 * (n0 + G_COLS)].rearrange("q (n t) -> q n t", t=4),
                        in0=src[:, :, n0:n0 + G_COLS].rearrange("q t n -> q n t"),
                        scalar1=1.0, scalar2=0.0, op0=ALU.mult, op1=ALU.add,
                    )
            else:
                dst = gb[:, 2048 * h:2048 * (h + 1)].rearrange("q (c i t) -> q c t i", i=4, t=4)
                s4 = src[:, :, 512 * h:512 * (h + 1)].rearrange("q t (c i) -> q c t i", i=4)
                if eng == "s":
                    nc.scalar.copy(out=dst, in_=s4)
                else:
                    nc.vector.tensor_copy(out=dst, in_=s4)

        def quant_b(i, g):
            if g == 0:
                state["bc", i] = codes.tile([P, 2048], U32, tag="bc", name="bc_%d" % i, align_bytes=64)
                state["bsc", i] = codes.tile([P, 2048], U8, tag="bsc", name="bsc_%d" % i, align_bytes=64)
            nc.vector.quantize_mx(
                out=state["bc", i][:, 1024 * g:1024 * (g + 1)].bitcast(FP8X4),
                scales=state["bsc", i][:, 1024 * g:1024 * (g + 1)],
                in_=state["gb", i, g][:],
            )

        def multiply(i, j):
            if j % 2 == 0:
                state["o", i, j // 2] = outp.tile([P, 2048], F32, tag="o", name="o_%d_%d" % (i, j // 2))
            o_t = state["o", i, j // 2]
            for h in range(2):
                acc = ps_acc.tile([P, 512], F32, tag="acc", name="acc_%d_%d_%d" % (i, j, h))
                for g in range(2):
                    lo = 256 * j + 128 * g
                    ro = 1024 * g + 512 * h
                    nc.tensor.matmul_mx(
                        out=acc[:],
                        lhsT=state["ac", i][:, lo:lo + 128].bitcast(FP8X4),
                        lhsT_scale=state["asc", i][:, lo:lo + 128],
                        rhs=state["bc", i][:, ro:ro + 512].bitcast(FP8X4),
                        rhs_scale=state["bsc", i][:, ro:ro + 512],
                        start=(g == 0),
                        stop=(g == 1),
                    )
                oo = 1024 * (j % 2) + 512 * h
                copy = nc.vector.tensor_copy if (i == NB - 1 and h == 1) else nc.scalar.copy
                copy(out=o_t[:, oo:oo + 512], in_=acc[:])
            if j % 2 == 1:
                c = j // 2
                nc.sync.dma_start(
                    out=out[i].rearrange("(p j) n -> p (j n)", j=8)[:, 2048 * c:2048 * (c + 1)], in_=o_t[:]
                )

        def regroup_batch(i, eng):
            for (g, h), e in zip(((0, 0), (0, 1), (1, 0), (1, 1)), RG[i]):
                if e == eng:
                    regroup(i, g, h, e)

        absmax(0, 0)
        absmax(0, 1)
        chain_a(0)
        count(0)
        regroup_batch(0, "s")
        regroup_batch(0, "v")
        chain_b(0)
        mask_mul(0)
        for i in range(NB):
            more = i + 1 < NB
            for j in range(8):
                transposes(i, j)
                exit_a(i, j)
            if more:
                absmax(i + 1, 0)
                regroup_batch(i + 1, "s")
            quant_b(i, 0)
            quant_b(i, 1)
            quant_a(i, 0)
            quant_a(i, 1)
            if more:
                for j in range(4):
                    multiply(i, j)
                absmax(i + 1, 1)
                chain_a(i + 1)
                count(i + 1)
                regroup_batch(i + 1, "v")
            quant_a(i, 2)
            quant_a(i, 3)
            if more:
                chain_b(i + 1)
                mask_mul(i + 1)
            for j in range(4 if more else 0, 8):
                multiply(i, j)


RG = (("s", "s", "s", "v"), ("v", "s", "v", "s"), ("v", "s", "v", "s"), ("v", "s", "v", "s"))
